import numpy as np
import ml_dtypes


def mxq(x, axis, fmt="e4m3"):
    dtype, down = {"e4m3": (ml_dtypes.float8_e4m3fn, 7), "e5m2": (ml_dtypes.float8_e5m2, 14)}[fmt]
    v = np.moveaxis(np.asarray(x, np.float32).astype(ml_dtypes.bfloat16).astype(np.float64), axis, -1)
    blocks = v.reshape(v.shape[:-1] + (-1, 32))
    amax = np.abs(blocks).max(-1, keepdims=True)
    byte = np.maximum(np.where(amax > 0, np.frexp(amax)[1] - 1 + 127, 0) - down, 1)
    scale = np.exp2(byte - 127.0)
    codes = (blocks / scale).astype(np.float32).astype(dtype).astype(np.float64)
    return np.moveaxis((codes * scale).reshape(v.shape), -1, axis)


WIDE = False


def mx_kscale(k):
    if not WIDE:
        return np.ones(k)
    levels = np.array([10, -10, 5, -5, 0])
    if k % 512:
        return np.exp2(np.random.permutation(np.resize(levels, k // 32))).repeat(32)
    a = np.empty((k // 512, 16))
    for p in range(k // 512):
        a[p, :8] = np.random.permutation(np.resize(levels, 8))
        for g in range(8):
            far = levels[np.abs(levels - a[p, g]) >= 10]
            a[p, g + 8] = far[np.random.randint(len(far))]
    return np.exp2(a.ravel()).repeat(32)


BF16 = ml_dtypes.bfloat16


def bf(x):
    return np.asarray(x, np.float32).astype(BF16)


def f64(x):
    return np.asarray(x).astype(np.float64)


U, I, D = 8192, 256, 512
C = 1.0
EPS = 1e-7
MAX_SQDIST = 50.0


def setup_inputs():
    s = mx_kscale(D)
    a = np.sqrt(600.0 / np.sqrt(D))
    hu = np.random.standard_normal((U, D)) * a * s
    hi = np.random.standard_normal((I, D)) * a / s
    return {"h": bf(np.concatenate([hu, hi], 0))}


def reference(h):
    h = f64(h)
    hu = h[:U]
    hi = h[U:U + I]
    signs = np.concatenate([-np.ones(1), np.ones(D - 1)])
    prod = mxq(hu, 1, "e4m3") @ mxq(hi * signs, 1, "e4m3").T
    K = 1.0 / C
    theta = np.maximum(-prod / K, 1.0 + EPS)
    sqdist = np.minimum(K * np.arccosh(theta) ** 2, MAX_SQDIST)
    return -sqdist

@@ -1,0 +1,175 @@
+import math
+from contextlib import ExitStack
+
+import concourse.mybir as mybir
+from concourse.masks import make_identity
+
+F32 = mybir.dt.float32
+BF16 = mybir.dt.bfloat16
+U32 = mybir.dt.uint32
+U8 = mybir.dt.uint8
+FP8X4 = mybir.dt.float8_e4m3fn_x4
+ALU = mybir.AluOpType
+ACT = mybir.ActivationFunctionType
+
+P = 128
+USERS, ITEMS, COORDS = 8192, 256, 512
+FLOPS = 2 * USERS * ITEMS * COORDS
+
+WORDS = COORDS // 2
+HALVES = WORDS // P
+USER_TILES = USERS // P
+ITEM_TILES = ITEMS // P
+TILES_PER_BANK = 2
+BANKS_PER_GROUP = 2
+GROUP = TILES_PER_BANK * BANKS_PER_GROUP
+N_GROUPS = USER_TILES // GROUP
+GROUP_COLS = GROUP * ITEMS
+
+THETA_MIN = 1.0 + 1e-7
+MAX_SQDIST = 50.0
+THETA_MAX = 0.5 * (math.exp(math.sqrt(MAX_SQDIST)) + math.exp(-math.sqrt(MAX_SQDIST)))
+
+
+def tile_hgatmodel_t_kernel(tc, h, out):
+    nc = tc.nc
+    users_in = h[0:USERS, :].rearrange("(p t) d -> p (t d)", t=USER_TILES)
+    items_in = h[USERS : USERS + ITEMS, :].rearrange("(j p) d -> p j d", p=P)
+    result_out = out.rearrange("(p t) i -> p (t i)", t=USER_TILES)
+
+    with ExitStack() as ctx:
+        consts = ctx.enter_context(tc.tile_pool(name="consts", bufs=1))
+        rows = ctx.enter_context(tc.tile_pool(name="rows", bufs=N_GROUPS))
+        stage = ctx.enter_context(tc.tile_pool(name="stage", bufs=3))
+        thetas = ctx.enter_context(tc.tile_pool(name="thetas", bufs=6))
+        results = ctx.enter_context(tc.tile_pool(name="results", bufs=N_GROUPS))
+        flipped = ctx.enter_context(tc.psum_pool(name="flipped", bufs=4))
+        products = ctx.enter_context(tc.psum_pool(name="products", bufs=4))
+        ctx.enter_context(tc.manual_schedule())
+
+        item_rows = consts.tile([P, ITEM_TILES * COORDS], BF16)
+        nc.sync.dma_start(out=item_rows[:].rearrange("p (j d) -> p j d", j=ITEM_TILES), in_=items_in)
+        user_rows = {}
+        for g in range(N_GROUPS):
+            user_rows[g] = rows.tile([P, GROUP * COORDS], BF16, name="user_rows")
+            nc.sync.dma_start(
+                out=user_rows[g][:], in_=users_in[:, g * GROUP * COORDS : (g + 1) * GROUP * COORDS]
+            )
+
+        identity = consts.tile([P, P], F32)
+        make_identity(nc, identity[:])
+        minus_one = consts.tile([P, 1], F32)
+        nc.vector.memset(minus_one[:], -1.0)
+        table_warmer = consts.tile([P, 1], F32)
+        nc.scalar.activation(out=table_warmer[:], in_=minus_one[:], func=ACT.Sqrt, scale=-1.0)
+
+        def transpose_tiles(source, n_tiles):
+            words = source[:].bitcast(F32)
+            banks = []
+            for b in range(n_tiles // TILES_PER_BANK):
+                bank = flipped.tile([P, TILES_PER_BANK, HALVES, P], F32, name="bank")
+                for t in range(TILES_PER_BANK):
+                    for u in range(HALVES):
+                        first = (b * TILES_PER_BANK + t) * WORDS
+                        nc.tensor.transpose(
+                            bank[:, t, u, :], words[:, first + u : first + WORDS : HALVES], identity[:]
+                        )
+                banks.append(bank)
+            return banks
+
+        def regroup(copy, bank, grouped, b):
+            as_words = grouped[:].bitcast(F32).rearrange("p (t r u) -> p t r u", r=P, u=HALVES)
+            copy(
+                out=as_words[:, b * TILES_PER_BANK : (b + 1) * TILES_PER_BANK],
+                in_=bank[:].rearrange("p t u r -> p t r u"),
+            )
+
+        def quantise(pool, grouped, n_tiles):
+            codes = pool.tile([P, n_tiles * P], U32, name="codes%d" % n_tiles, align_bytes=64)
+            scales = pool.tile([P, n_tiles * P], U8, name="scales%d" % n_tiles, align_bytes=64)
+            nc.vector.quantize_mx(out=codes[:].bitcast(FP8X4), scales=scales[:], in_=grouped[:])
+            return codes, scales
+
+        first_coord = item_rows[:].rearrange("p (j d) -> p j d", j=ITEM_TILES)[:, :, 0:1]
+        nc.vector.tensor_scalar(out=first_coord, in0=first_coord, scalar1=-1.0, scalar2=None, op0=ALU.mult)
+        item_banks = transpose_tiles(item_rows, ITEM_TILES)
+        item_grouped = consts.tile([P, ITEM_TILES * COORDS], BF16, align_bytes=64)
+        regroup(nc.vector.tensor_copy, item_banks[0], item_grouped, 0)
+        item_codes, item_scales = quantise(consts, item_grouped, ITEM_TILES)
+
+        banks_of, grouped_of, quantised_of, product_of, theta_of, work_of = {}, {}, {}, {}, {}, {}
+
+        def transpose_users(g):
+            banks_of[g] = transpose_tiles(user_rows[g], GROUP)
+
+        def regroup_users(g):
+            grouped_of[g] = stage.tile([P, GROUP * COORDS], BF16, name="grouped", align_bytes=64)
+            for b in range(BANKS_PER_GROUP):
+                on_vector = (g * BANKS_PER_GROUP + b) % 4 == 3
+                regroup(nc.vector.tensor_copy if on_vector else nc.scalar.copy, banks_of[g][b], grouped_of[g], b)
+
+        def quantise_users(g):
+            quantised_of[g] = quantise(stage, grouped_of[g], GROUP)
+
+        def multiply(g):
+            codes, scales = quantised_of[g]
+            product_of[g] = []
+            for b in range(BANKS_PER_GROUP):
+                bank = products.tile([P, TILES_PER_BANK, ITEMS], F32, name="product")
+                for t in range(TILES_PER_BANK):
+                    cols = slice((b * TILES_PER_BANK + t) * P, (b * TILES_PER_BANK + t + 1) * P)
+                    nc.tensor.matmul_mx(
+                        out=bank[:, t, :],
+                        lhsT=codes[:, cols].bitcast(FP8X4),
+                        lhsT_scale=scales[:, cols],
+                        rhs=item_codes[:].bitcast(FP8X4),
+                        rhs_scale=item_scales[:],
+                        start=True,
+                        stop=True,
+                    )
+                product_of[g].append(bank)
+
+        def clamp(g):
+            theta_of[g] = thetas.tile([P, GROUP_COLS], F32, name="minus_theta")
+            width = TILES_PER_BANK * ITEMS
+            for b in range(BANKS_PER_GROUP):
+                nc.vector.tensor_scalar(
+                    out=theta_of[g][:, b * width : (b + 1) * width],
+                    in0=product_of[g][b][:].rearrange("p t i -> p (t i)"),
+                    scalar1=-THETA_MIN,
+                    scalar2=-THETA_MAX,
+                    op0=ALU.min,
+                    op1=ALU.max,
+                )
+
+        def square(g):
+            work_of[g] = results.tile([P, GROUP_COLS], F32, name="work")
+            nc.scalar.activation(out=work_of[g][:], in_=theta_of[g][:], func=ACT.Square)
+
+        def root(g):
+            nc.scalar.activation(out=work_of[g][:], in_=work_of[g][:], func=ACT.Sqrt, bias=minus_one[:], scale=1.0)
+
+        def add_theta(g):
+            nc.vector.tensor_tensor(out=work_of[g][:], in0=work_of[g][:], in1=theta_of[g][:], op=ALU.subtract)
+
+        def run(stage_fn, g):
+            if 0 <= g < N_GROUPS:
+                stage_fn(g)
+
+        LAST_LAG = 7
+        for step in range(N_GROUPS + LAST_LAG):
+            run(transpose_users, step)
+            run(quantise_users, step - 2)
+            run(multiply, step - 2)
+            run(clamp, step - 3)
+            run(regroup_users, step - 1)
+            run(square, step - 4)
+            run(root, step - 5)
+            run(add_theta, step - LAST_LAG)
+
+        for g in range(N_GROUPS):
+            nc.scalar.activation(out=work_of[g][:], in_=work_of[g][:], func=ACT.Ln)
+            nc.vector.scalar_tensor_tensor(
+                out=work_of[g][:], in0=work_of[g][:], scalar=-1.0, in1=work_of[g][:], op0=ALU.mult, op1=ALU.mult
+            )
+            nc.sync.dma_start(out=result_out[:, g * GROUP_COLS : (g + 1) * GROUP_COLS], in_=work_of[g][:])

@@ -21,10 +21,12 @@ HALVES = WORDS // P
 USER_TILES = USERS // P
 ITEM_TILES = ITEMS // P
 TILES_PER_BANK = 2
-BANKS_PER_GROUP = 2
-GROUP = TILES_PER_BANK * BANKS_PER_GROUP
-N_GROUPS = USER_TILES // GROUP
-GROUP_COLS = GROUP * ITEMS
+BANK_ROWS = TILES_PER_BANK * COORDS
+BANK_COLS = TILES_PER_BANK * ITEMS
+GROUP_BANKS = [1, 1] + [2] * (USER_TILES // TILES_PER_BANK // 2 - 2) + [1, 1]
+N_GROUPS = len(GROUP_BANKS)
+FIRST_BANK = [sum(GROUP_BANKS[:g]) for g in range(N_GROUPS)]
+MAX_BANKS = max(GROUP_BANKS)
 
 THETA_MIN = 1.0 + 1e-7
 MAX_SQDIST = 50.0
@@ -39,22 +41,22 @@ def tile_hgatmodel_t_kernel(tc, h, out):
 
     with ExitStack() as ctx:
         consts = ctx.enter_context(tc.tile_pool(name="consts", bufs=1))
-        rows = ctx.enter_context(tc.tile_pool(name="rows", bufs=N_GROUPS))
+        rows = ctx.enter_context(tc.tile_pool(name="rows", bufs=1))
         stage = ctx.enter_context(tc.tile_pool(name="stage", bufs=3))
         thetas = ctx.enter_context(tc.tile_pool(name="thetas", bufs=6))
-        results = ctx.enter_context(tc.tile_pool(name="results", bufs=N_GROUPS))
+        results = ctx.enter_context(tc.tile_pool(name="results", bufs=1))
         flipped = ctx.enter_context(tc.psum_pool(name="flipped", bufs=4))
         products = ctx.enter_context(tc.psum_pool(name="products", bufs=4))
         ctx.enter_context(tc.manual_schedule())
 
         item_rows = consts.tile([P, ITEM_TILES * COORDS], BF16)
-        nc.sync.dma_start(out=item_rows[:].rearrange("p (j d) -> p j d", j=ITEM_TILES), in_=items_in)
         user_rows = {}
         for g in range(N_GROUPS):
-            user_rows[g] = rows.tile([P, GROUP * COORDS], BF16, name="user_rows")
-            nc.sync.dma_start(
-                out=user_rows[g][:], in_=users_in[:, g * GROUP * COORDS : (g + 1) * GROUP * COORDS]
-            )
+            first, width = FIRST_BANK[g] * BANK_ROWS, GROUP_BANKS[g] * BANK_ROWS
+            user_rows[g] = rows.tile([P, width], BF16, name="user_rows%d" % g)
+            nc.sync.dma_start(out=user_rows[g][:], in_=users_in[:, first : first + width])
+            if g == 0:
+                nc.sync.dma_start(out=item_rows[:].rearrange("p (j d) -> p j d", j=ITEM_TILES), in_=items_in)
 
         identity = consts.tile([P, P], F32)
         make_identity(nc, identity[:])
@@ -90,31 +92,32 @@ def tile_hgatmodel_t_kernel(tc, h, out):
             nc.vector.quantize_mx(out=codes[:].bitcast(FP8X4), scales=scales[:], in_=grouped[:])
             return codes, scales
 
-        first_coord = item_rows[:].rearrange("p (j d) -> p j d", j=ITEM_TILES)[:, :, 0:1]
-        nc.vector.tensor_scalar(out=first_coord, in0=first_coord, scalar1=-1.0, scalar2=None, op0=ALU.mult)
-        item_banks = transpose_tiles(item_rows, ITEM_TILES)
-        item_grouped = consts.tile([P, ITEM_TILES * COORDS], BF16, align_bytes=64)
-        regroup(nc.vector.tensor_copy, item_banks[0], item_grouped, 0)
-        item_codes, item_scales = quantise(consts, item_grouped, ITEM_TILES)
+        def prepare_items():
+            first_coord = item_rows[:].rearrange("p (j d) -> p j d", j=ITEM_TILES)[:, :, 0:1]
+            nc.vector.tensor_scalar(out=first_coord, in0=first_coord, scalar1=-1.0, scalar2=None, op0=ALU.mult)
+            bank = transpose_tiles(item_rows, ITEM_TILES)[0]
+            grouped = consts.tile([P, ITEM_TILES * COORDS], BF16, name="item_grouped", align_bytes=64)
+            regroup(nc.vector.tensor_copy, bank, grouped, 0)
+            return quantise(consts, grouped, ITEM_TILES)
 
         banks_of, grouped_of, quantised_of, product_of, theta_of, work_of = {}, {}, {}, {}, {}, {}
 
         def transpose_users(g):
-            banks_of[g] = transpose_tiles(user_rows[g], GROUP)
+            banks_of[g] = transpose_tiles(user_rows[g], GROUP_BANKS[g] * TILES_PER_BANK)
 
         def regroup_users(g):
-            grouped_of[g] = stage.tile([P, GROUP * COORDS], BF16, name="grouped", align_bytes=64)
-            for b in range(BANKS_PER_GROUP):
-                on_vector = (g * BANKS_PER_GROUP + b) % 4 == 3
+            grouped_of[g] = stage.tile([P, GROUP_BANKS[g] * BANK_ROWS], BF16, name="grouped", align_bytes=64)
+            for b in range(GROUP_BANKS[g]):
+                on_vector = (FIRST_BANK[g] + b) % 4 == 3
                 regroup(nc.vector.tensor_copy if on_vector else nc.scalar.copy, banks_of[g][b], grouped_of[g], b)
 
         def quantise_users(g):
-            quantised_of[g] = quantise(stage, grouped_of[g], GROUP)
+            quantised_of[g] = quantise(stage, grouped_of[g], GROUP_BANKS[g] * TILES_PER_BANK)
 
         def multiply(g):
             codes, scales = quantised_of[g]
             product_of[g] = []
-            for b in range(BANKS_PER_GROUP):
+            for b in range(GROUP_BANKS[g]):
                 bank = products.tile([P, TILES_PER_BANK, ITEMS], F32, name="product")
                 for t in range(TILES_PER_BANK):
                     cols = slice((b * TILES_PER_BANK + t) * P, (b * TILES_PER_BANK + t + 1) * P)
@@ -130,11 +133,10 @@ def tile_hgatmodel_t_kernel(tc, h, out):
                 product_of[g].append(bank)
 
         def clamp(g):
-            theta_of[g] = thetas.tile([P, GROUP_COLS], F32, name="minus_theta")
-            width = TILES_PER_BANK * ITEMS
-            for b in range(BANKS_PER_GROUP):
+            theta_of[g] = thetas.tile([P, GROUP_BANKS[g] * BANK_COLS], F32, name="minus_theta")
+            for b in range(GROUP_BANKS[g]):
                 nc.vector.tensor_scalar(
-                    out=theta_of[g][:, b * width : (b + 1) * width],
+                    out=theta_of[g][:, b * BANK_COLS : (b + 1) * BANK_COLS],
                     in0=product_of[g][b][:].rearrange("p t i -> p (t i)"),
                     scalar1=-THETA_MIN,
                     scalar2=-THETA_MAX,
@@ -143,7 +145,7 @@ def tile_hgatmodel_t_kernel(tc, h, out):
                 )
 
         def square(g):
-            work_of[g] = results.tile([P, GROUP_COLS], F32, name="work")
+            work_of[g] = results.tile([P, GROUP_BANKS[g] * BANK_COLS], F32, name="work%d" % g)
             nc.scalar.activation(out=work_of[g][:], in_=theta_of[g][:], func=ACT.Square)
 
         def root(g):
@@ -159,6 +161,8 @@ def tile_hgatmodel_t_kernel(tc, h, out):
         LAST_LAG = 7
         for step in range(N_GROUPS + LAST_LAG):
             run(transpose_users, step)
+            if step == 0:
+                item_codes, item_scales = prepare_items()
             run(quantise_users, step - 2)
             run(multiply, step - 2)
             run(clamp, step - 3)
@@ -172,4 +176,5 @@ def tile_hgatmodel_t_kernel(tc, h, out):
             nc.vector.scalar_tensor_tensor(
                 out=work_of[g][:], in0=work_of[g][:], scalar=-1.0, in1=work_of[g][:], op0=ALU.mult, op1=ALU.mult
             )
-            nc.sync.dma_start(out=result_out[:, g * GROUP_COLS : (g + 1) * GROUP_COLS], in_=work_of[g][:])
+            first, width = FIRST_BANK[g] * BANK_COLS, GROUP_BANKS[g] * BANK_COLS
+            nc.sync.dma_start(out=result_out[:, first : first + width], in_=work_of[g][:])

@@ -27,6 +27,7 @@ GROUP_BANKS = [1, 1] + [2] * (USER_TILES // TILES_PER_BANK // 2 - 2) + [1, 1]
 N_GROUPS = len(GROUP_BANKS)
 FIRST_BANK = [sum(GROUP_BANKS[:g]) for g in range(N_GROUPS)]
 MAX_BANKS = max(GROUP_BANKS)
+SCALAR_BANKS = 8
 
 THETA_MIN = 1.0 + 1e-7
 MAX_SQDIST = 50.0
@@ -43,7 +44,7 @@ def tile_hgatmodel_t_kernel(tc, h, out):
         consts = ctx.enter_context(tc.tile_pool(name="consts", bufs=1))
         rows = ctx.enter_context(tc.tile_pool(name="rows", bufs=1))
         stage = ctx.enter_context(tc.tile_pool(name="stage", bufs=3))
-        thetas = ctx.enter_context(tc.tile_pool(name="thetas", bufs=6))
+        thetas = ctx.enter_context(tc.tile_pool(name="thetas", bufs=1))
         results = ctx.enter_context(tc.tile_pool(name="results", bufs=1))
         flipped = ctx.enter_context(tc.psum_pool(name="flipped", bufs=4))
         products = ctx.enter_context(tc.psum_pool(name="products", bufs=4))
@@ -108,7 +109,8 @@ def tile_hgatmodel_t_kernel(tc, h, out):
         def regroup_users(g):
             grouped_of[g] = stage.tile([P, GROUP_BANKS[g] * BANK_ROWS], BF16, name="grouped", align_bytes=64)
             for b in range(GROUP_BANKS[g]):
-                on_vector = (FIRST_BANK[g] + b) % 4 == 3
+                bank_index = FIRST_BANK[g] + b
+                on_vector = bank_index >= SCALAR_BANKS and bank_index % 2 == 1
                 regroup(nc.vector.tensor_copy if on_vector else nc.scalar.copy, banks_of[g][b], grouped_of[g], b)
 
         def quantise_users(g):
@@ -133,7 +135,7 @@ def tile_hgatmodel_t_kernel(tc, h, out):
                 product_of[g].append(bank)
 
         def clamp(g):
-            theta_of[g] = thetas.tile([P, GROUP_BANKS[g] * BANK_COLS], F32, name="minus_theta")
+            theta_of[g] = thetas.tile([P, GROUP_BANKS[g] * BANK_COLS], F32, name="minus_theta%d" % g)
             for b in range(GROUP_BANKS[g]):
                 nc.vector.tensor_scalar(
                     out=theta_of[g][:, b * BANK_COLS : (b + 1) * BANK_COLS],
@@ -152,27 +154,38 @@ def tile_hgatmodel_t_kernel(tc, h, out):
             nc.scalar.activation(out=work_of[g][:], in_=work_of[g][:], func=ACT.Sqrt, bias=minus_one[:], scale=1.0)
 
         def add_theta(g):
-            nc.vector.tensor_tensor(out=work_of[g][:], in0=work_of[g][:], in1=theta_of[g][:], op=ALU.subtract)
+            ours = slice(0, BANK_COLS)
+            nc.vector.tensor_tensor(
+                out=work_of[g][:, ours], in0=work_of[g][:, ours], in1=theta_of[g][:, ours], op=ALU.subtract
+            )
+            if GROUP_BANKS[g] == MAX_BANKS:
+                theirs = slice(BANK_COLS, MAX_BANKS * BANK_COLS)
+                nc.gpsimd.tensor_tensor(
+                    out=theta_of[g][:, ours], in0=work_of[g][:, theirs], in1=theta_of[g][:, theirs], op=ALU.subtract
+                )
 
         def run(stage_fn, g):
             if 0 <= g < N_GROUPS:
                 stage_fn(g)
 
-        LAST_LAG = 7
+        LAST_LAG = 6
         for step in range(N_GROUPS + LAST_LAG):
             run(transpose_users, step)
             if step == 0:
                 item_codes, item_scales = prepare_items()
             run(quantise_users, step - 2)
-            run(multiply, step - 2)
-            run(clamp, step - 3)
-            run(regroup_users, step - 1)
-            run(square, step - 4)
-            run(root, step - 5)
             run(add_theta, step - LAST_LAG)
+            run(multiply, step - 2)
+            run(regroup_users, step - 1)
+            run(clamp, step - 3)
+            run(root, step - 5)
+            run(square, step - 4)
 
         for g in range(N_GROUPS):
-            nc.scalar.activation(out=work_of[g][:], in_=work_of[g][:], func=ACT.Ln)
+            ours = slice(0, BANK_COLS)
+            nc.scalar.activation(out=work_of[g][:, ours], in_=work_of[g][:, ours], func=ACT.Ln)
+            if GROUP_BANKS[g] == MAX_BANKS:
+                nc.scalar.activation(out=work_of[g][:, BANK_COLS:], in_=theta_of[g][:, ours], func=ACT.Ln)
             nc.vector.scalar_tensor_tensor(
                 out=work_of[g][:], in0=work_of[g][:], scalar=-1.0, in1=work_of[g][:], op0=ALU.mult, op1=ALU.mult
             )

@@ -23,11 +23,17 @@ ITEM_TILES = ITEMS // P
 TILES_PER_BANK = 2
 BANK_ROWS = TILES_PER_BANK * COORDS
 BANK_COLS = TILES_PER_BANK * ITEMS
-GROUP_BANKS = [1, 1] + [2] * (USER_TILES // TILES_PER_BANK // 2 - 2) + [1, 1]
+GROUP_BANKS = [1, 1] + [2] * (USER_TILES // TILES_PER_BANK // 2 - 1)
 N_GROUPS = len(GROUP_BANKS)
 FIRST_BANK = [sum(GROUP_BANKS[:g]) for g in range(N_GROUPS)]
 MAX_BANKS = max(GROUP_BANKS)
-SCALAR_BANKS = 8
+REGROUP_LAG, QUANTISE_LAG, CLAMP_LAG, SQUARE_LAG, ROOT_LAG, ADD_LAG = 1, 2, 3, 4, 5, 7
+SCALAR_BANKS = 6
+VECTOR_COLS = 256
+OVERLAP = 8
+VECTOR_ADD_GROUPS = 4
+VECTOR_SQUARE_GROUPS = 1
+END_COLS = 256
 
 THETA_MIN = 1.0 + 1e-7
 MAX_SQDIST = 50.0
@@ -44,7 +50,8 @@ def tile_hgatmodel_t_kernel(tc, h, out):
         consts = ctx.enter_context(tc.tile_pool(name="consts", bufs=1))
         rows = ctx.enter_context(tc.tile_pool(name="rows", bufs=1))
         stage = ctx.enter_context(tc.tile_pool(name="stage", bufs=3))
-        thetas = ctx.enter_context(tc.tile_pool(name="thetas", bufs=1))
+        thetas = ctx.enter_context(tc.tile_pool(name="thetas", bufs=ADD_LAG - CLAMP_LAG + 2))
+        roots = ctx.enter_context(tc.tile_pool(name="roots", bufs=ADD_LAG - SQUARE_LAG + 2))
         results = ctx.enter_context(tc.tile_pool(name="results", bufs=1))
         flipped = ctx.enter_context(tc.psum_pool(name="flipped", bufs=4))
         products = ctx.enter_context(tc.psum_pool(name="products", bufs=4))
@@ -101,7 +108,8 @@ def tile_hgatmodel_t_kernel(tc, h, out):
             regroup(nc.vector.tensor_copy, bank, grouped, 0)
             return quantise(consts, grouped, ITEM_TILES)
 
-        banks_of, grouped_of, quantised_of, product_of, theta_of, work_of = {}, {}, {}, {}, {}, {}
+        banks_of, grouped_of, quantised_of, product_of, theta_of, root_of = {}, {}, {}, {}, {}, {}
+        result_of = {}
 
         def transpose_users(g):
             banks_of[g] = transpose_tiles(user_rows[g], GROUP_BANKS[g] * TILES_PER_BANK)
@@ -135,7 +143,7 @@ def tile_hgatmodel_t_kernel(tc, h, out):
                 product_of[g].append(bank)
 
         def clamp(g):
-            theta_of[g] = thetas.tile([P, GROUP_BANKS[g] * BANK_COLS], F32, name="minus_theta%d" % g)
+            theta_of[g] = thetas.tile([P, GROUP_BANKS[g] * BANK_COLS], F32, name="minus_theta")
             for b in range(GROUP_BANKS[g]):
                 nc.vector.tensor_scalar(
                     out=theta_of[g][:, b * BANK_COLS : (b + 1) * BANK_COLS],
@@ -147,47 +155,67 @@ def tile_hgatmodel_t_kernel(tc, h, out):
                 )
 
         def square(g):
-            work_of[g] = results.tile([P, GROUP_BANKS[g] * BANK_COLS], F32, name="work%d" % g)
-            nc.scalar.activation(out=work_of[g][:], in_=theta_of[g][:], func=ACT.Square)
+            root_of[g] = roots.tile([P, GROUP_BANKS[g] * BANK_COLS], F32, name="root")
+            if g >= N_GROUPS - VECTOR_SQUARE_GROUPS:
+                for b in range(GROUP_BANKS[g]):
+                    cols = slice(b * BANK_COLS, (b + 1) * BANK_COLS)
+                    theta = theta_of[g][:, cols]
+                    nc.vector.tensor_tensor(out=root_of[g][:, cols], in0=theta, in1=theta, op=ALU.mult)
+            else:
+                nc.scalar.activation(out=root_of[g][:], in_=theta_of[g][:], func=ACT.Square)
 
         def root(g):
-            nc.scalar.activation(out=work_of[g][:], in_=work_of[g][:], func=ACT.Sqrt, bias=minus_one[:], scale=1.0)
+            nc.scalar.activation(out=root_of[g][:], in_=root_of[g][:], func=ACT.Sqrt, bias=minus_one[:], scale=1.0)
 
         def add_theta(g):
-            ours = slice(0, BANK_COLS)
-            nc.vector.tensor_tensor(
-                out=work_of[g][:, ours], in0=work_of[g][:, ours], in1=theta_of[g][:, ours], op=ALU.subtract
-            )
-            if GROUP_BANKS[g] == MAX_BANKS:
-                theirs = slice(BANK_COLS, MAX_BANKS * BANK_COLS)
-                nc.gpsimd.tensor_tensor(
-                    out=theta_of[g][:, ours], in0=work_of[g][:, theirs], in1=theta_of[g][:, theirs], op=ALU.subtract
+            cols = GROUP_BANKS[g] * BANK_COLS
+            result_of[g] = results.tile([P, cols], F32, name="result%d" % g)
+            shared = GROUP_BANKS[g] == MAX_BANKS and g < N_GROUPS - VECTOR_ADD_GROUPS
+            parts = [(nc.vector, 0, VECTOR_COLS + OVERLAP if shared else cols)]
+            if shared:
+                parts.append((nc.gpsimd, VECTOR_COLS, cols))
+            for engine, first, last in parts:
+                engine.tensor_tensor(
+                    out=result_of[g][:, first:last],
+                    in0=root_of[g][:, first:last],
+                    in1=theta_of[g][:, first:last],
+                    op=ALU.subtract,
                 )
 
         def run(stage_fn, g):
             if 0 <= g < N_GROUPS:
                 stage_fn(g)
 
-        LAST_LAG = 6
-        for step in range(N_GROUPS + LAST_LAG):
+        for step in range(N_GROUPS + ADD_LAG):
             run(transpose_users, step)
             if step == 0:
                 item_codes, item_scales = prepare_items()
-            run(quantise_users, step - 2)
-            run(add_theta, step - LAST_LAG)
-            run(multiply, step - 2)
-            run(regroup_users, step - 1)
-            run(clamp, step - 3)
-            run(root, step - 5)
-            run(square, step - 4)
+            run(quantise_users, step - QUANTISE_LAG)
+            run(multiply, step - QUANTISE_LAG)
+            run(add_theta, step - ADD_LAG)
+            run(regroup_users, step - REGROUP_LAG)
+            run(clamp, step - CLAMP_LAG)
+            if step - CLAMP_LAG >= N_GROUPS - VECTOR_SQUARE_GROUPS:
+                run(square, step - CLAMP_LAG)
+            if step - SQUARE_LAG < N_GROUPS - VECTOR_SQUARE_GROUPS:
+                run(square, step - SQUARE_LAG)
+            run(root, step - ROOT_LAG)
+
+        def pieces(g):
+            cols = GROUP_BANKS[g] * BANK_COLS
+            cuts = [0, cols]
+            if g == 0:
+                cuts = list(range(0, cols + 1, END_COLS))
+            if g == N_GROUPS - 1:
+                cuts = [0] + list(range(cols - BANK_COLS, cols + 1, END_COLS))
+            return list(zip(cuts[:-1], cuts[1:]))
 
         for g in range(N_GROUPS):
-            ours = slice(0, BANK_COLS)
-            nc.scalar.activation(out=work_of[g][:, ours], in_=work_of[g][:, ours], func=ACT.Ln)
-            if GROUP_BANKS[g] == MAX_BANKS:
-                nc.scalar.activation(out=work_of[g][:, BANK_COLS:], in_=theta_of[g][:, ours], func=ACT.Ln)
-            nc.vector.scalar_tensor_tensor(
-                out=work_of[g][:], in0=work_of[g][:], scalar=-1.0, in1=work_of[g][:], op0=ALU.mult, op1=ALU.mult
-            )
-            first, width = FIRST_BANK[g] * BANK_COLS, GROUP_BANKS[g] * BANK_COLS
-            nc.sync.dma_start(out=result_out[:, first : first + width], in_=work_of[g][:])
+            for first, last in pieces(g):
+                part = result_of[g][:, first:last]
+                nc.scalar.activation(out=part, in_=part, func=ACT.Ln)
+                nc.vector.scalar_tensor_tensor(
+                    out=part, in0=part, scalar=-1.0, in1=part, op0=ALU.mult, op1=ALU.mult
+                )
+                offset = FIRST_BANK[g] * BANK_COLS
+                nc.sync.dma_start(out=result_out[:, offset + first : offset + last], in_=part)

@@ -27,11 +27,12 @@ GROUP_BANKS = [1, 1] + [2] * (USER_TILES // TILES_PER_BANK // 2 - 1)
 N_GROUPS = len(GROUP_BANKS)
 FIRST_BANK = [sum(GROUP_BANKS[:g]) for g in range(N_GROUPS)]
 MAX_BANKS = max(GROUP_BANKS)
-REGROUP_LAG, QUANTISE_LAG, CLAMP_LAG, SQUARE_LAG, ROOT_LAG, ADD_LAG = 1, 2, 3, 4, 5, 7
-SCALAR_BANKS = 6
-VECTOR_COLS = 256
+REGROUP_LAG, QUANTISE_LAG, CLAMP_LAG, SQUARE_LAG, ROOT_LAG, ADD_LAG = 1, 2, 3, 4, 6, 9
+SCALAR_BANKS = 8
+VECTOR_COLS = 416
 OVERLAP = 8
-VECTOR_ADD_GROUPS = 4
+GPSIMD_GROUPS = 11
+TENSOR_ADD_GROUPS = 3
 VECTOR_SQUARE_GROUPS = 1
 END_COLS = 256
 
@@ -68,6 +69,8 @@ def tile_hgatmodel_t_kernel(tc, h, out):
 
         identity = consts.tile([P, P], F32)
         make_identity(nc, identity[:])
+        minus_identity = consts.tile([P, P], F32)
+        nc.vector.tensor_scalar(out=minus_identity[:], in0=identity[:], scalar1=-1.0, scalar2=None, op0=ALU.mult)
         minus_one = consts.tile([P, 1], F32)
         nc.vector.memset(minus_one[:], -1.0)
         table_warmer = consts.tile([P, 1], F32)
@@ -109,7 +112,7 @@ def tile_hgatmodel_t_kernel(tc, h, out):
             return quantise(consts, grouped, ITEM_TILES)
 
         banks_of, grouped_of, quantised_of, product_of, theta_of, root_of = {}, {}, {}, {}, {}, {}
-        result_of = {}
+        result_of, sum_of = {}, {}
 
         def transpose_users(g):
             banks_of[g] = transpose_tiles(user_rows[g], GROUP_BANKS[g] * TILES_PER_BANK)
@@ -118,7 +121,7 @@ def tile_hgatmodel_t_kernel(tc, h, out):
             grouped_of[g] = stage.tile([P, GROUP_BANKS[g] * BANK_ROWS], BF16, name="grouped", align_bytes=64)
             for b in range(GROUP_BANKS[g]):
                 bank_index = FIRST_BANK[g] + b
-                on_vector = bank_index >= SCALAR_BANKS and bank_index % 2 == 1
+                on_vector = bank_index >= SCALAR_BANKS and bank_index % 2 == 0
                 regroup(nc.vector.tensor_copy if on_vector else nc.scalar.copy, banks_of[g][b], grouped_of[g], b)
 
         def quantise_users(g):
@@ -170,7 +173,9 @@ def tile_hgatmodel_t_kernel(tc, h, out):
         def add_theta(g):
             cols = GROUP_BANKS[g] * BANK_COLS
             result_of[g] = results.tile([P, cols], F32, name="result%d" % g)
-            shared = GROUP_BANKS[g] == MAX_BANKS and g < N_GROUPS - VECTOR_ADD_GROUPS
+            if g >= N_GROUPS - TENSOR_ADD_GROUPS:
+                return
+            shared = GROUP_BANKS[g] == MAX_BANKS and g < GPSIMD_GROUPS
             parts = [(nc.vector, 0, VECTOR_COLS + OVERLAP if shared else cols)]
             if shared:
                 parts.append((nc.gpsimd, VECTOR_COLS, cols))
@@ -181,6 +186,15 @@ def tile_hgatmodel_t_kernel(tc, h, out):
                     in1=theta_of[g][:, first:last],
                     op=ALU.subtract,
                 )
+
+        def add_on_tensor(g):
+            for b in range(GROUP_BANKS[g]):
+                pool = flipped if b == 0 else products
+                bank = pool.tile([P, BANK_COLS], F32, name="bank" if b == 0 else "product")
+                cols = slice(b * BANK_COLS, (b + 1) * BANK_COLS)
+                nc.tensor.matmul(bank[:], lhsT=minus_identity[:], rhs=theta_of[g][:, cols], start=True, stop=False)
+                nc.tensor.matmul(bank[:], lhsT=identity[:], rhs=root_of[g][:, cols], start=False, stop=True)
+                sum_of[(g, b)] = bank
 
         def run(stage_fn, g):
             if 0 <= g < N_GROUPS:
@@ -193,13 +207,15 @@ def tile_hgatmodel_t_kernel(tc, h, out):
             run(quantise_users, step - QUANTISE_LAG)
             run(multiply, step - QUANTISE_LAG)
             run(add_theta, step - ADD_LAG)
+            run(root, step - ROOT_LAG)
             run(regroup_users, step - REGROUP_LAG)
             run(clamp, step - CLAMP_LAG)
             if step - CLAMP_LAG >= N_GROUPS - VECTOR_SQUARE_GROUPS:
                 run(square, step - CLAMP_LAG)
             if step - SQUARE_LAG < N_GROUPS - VECTOR_SQUARE_GROUPS:
                 run(square, step - SQUARE_LAG)
-            run(root, step - ROOT_LAG)
+        for g in range(N_GROUPS - TENSOR_ADD_GROUPS, N_GROUPS):
+            add_on_tensor(g)
 
         def pieces(g):
             cols = GROUP_BANKS[g] * BANK_COLS
@@ -212,10 +228,18 @@ def tile_hgatmodel_t_kernel(tc, h, out):
 
         for g in range(N_GROUPS):
             for first, last in pieces(g):
-                part = result_of[g][:, first:last]
-                nc.scalar.activation(out=part, in_=part, func=ACT.Ln)
-                nc.vector.scalar_tensor_tensor(
-                    out=part, in0=part, scalar=-1.0, in1=part, op0=ALU.mult, op1=ALU.mult
-                )
+                for start in range(first, last, BANK_COLS):
+                    stop = min(start + BANK_COLS, last)
+                    part = result_of[g][:, start:stop]
+                    source = part
+                    if g >= N_GROUPS - TENSOR_ADD_GROUPS:
+                        b = start // BANK_COLS
+                        source = sum_of[(g, b)][:, start - b * BANK_COLS : stop - b * BANK_COLS]
+                    nc.scalar.activation(out=part, in_=source, func=ACT.Ln)
+                    nc.vector.scalar_tensor_tensor(
+                        out=part, in0=part, scalar=-1.0, in1=part, op0=ALU.mult, op1=ALU.mult
+                    )
                 offset = FIRST_BANK[g] * BANK_COLS
-                nc.sync.dma_start(out=result_out[:, offset + first : offset + last], in_=part)
+                nc.sync.dma_start(
+                    out=result_out[:, offset + first : offset + last], in_=result_of[g][:, first:last]
+                )

@@ -32,7 +32,10 @@ SCALAR_BANKS = 8
 VECTOR_COLS = 416
 OVERLAP = 8
 GPSIMD_GROUPS = 11
-TENSOR_ADD_GROUPS = 3
+TENSOR_ADD_GROUPS = 2
+CLOCK_COLS = 96
+CLOCK_FIRST_GROUP = 5
+CLOCK_WARM_UPS = 3
 VECTOR_SQUARE_GROUPS = 1
 END_COLS = 256
 
@@ -69,6 +72,9 @@ def tile_hgatmodel_t_kernel(tc, h, out):
 
         identity = consts.tile([P, P], F32)
         make_identity(nc, identity[:])
+        warm_up = flipped.tile([P, TILES_PER_BANK, HALVES, P], F32, name="bank")
+        for i in range(CLOCK_WARM_UPS):
+            nc.tensor.matmul(warm_up[:, 0, i % HALVES, :], lhsT=identity[:], rhs=identity[:], start=True, stop=True)
         minus_identity = consts.tile([P, P], F32)
         nc.vector.tensor_scalar(out=minus_identity[:], in0=identity[:], scalar1=-1.0, scalar2=None, op0=ALU.mult)
         minus_one = consts.tile([P, 1], F32)
@@ -76,11 +82,15 @@ def tile_hgatmodel_t_kernel(tc, h, out):
         table_warmer = consts.tile([P, 1], F32)
         nc.scalar.activation(out=table_warmer[:], in_=minus_one[:], func=ACT.Sqrt, scale=-1.0)
 
-        def transpose_tiles(source, n_tiles):
+        def transpose_tiles(source, n_tiles, clock=False):
             words = source[:].bitcast(F32)
             banks = []
             for b in range(n_tiles // TILES_PER_BANK):
                 bank = flipped.tile([P, TILES_PER_BANK, HALVES, P], F32, name="bank")
+                if clock and b == 0:
+                    nc.tensor.matmul(
+                        bank[:, 0, 0, 0:CLOCK_COLS], lhsT=identity[:], rhs=identity[:, 0:CLOCK_COLS], start=True, stop=True
+                    )
                 for t in range(TILES_PER_BANK):
                     for u in range(HALVES):
                         first = (b * TILES_PER_BANK + t) * WORDS
@@ -115,7 +125,7 @@ def tile_hgatmodel_t_kernel(tc, h, out):
         result_of, sum_of = {}, {}
 
         def transpose_users(g):
-            banks_of[g] = transpose_tiles(user_rows[g], GROUP_BANKS[g] * TILES_PER_BANK)
+            banks_of[g] = transpose_tiles(user_rows[g], GROUP_BANKS[g] * TILES_PER_BANK, g >= CLOCK_FIRST_GROUP)
 
         def regroup_users(g):
             grouped_of[g] = stage.tile([P, GROUP_BANKS[g] * BANK_ROWS], BF16, name="grouped", align_bytes=64)

@@ -29,7 +29,7 @@ FIRST_BANK = [sum(GROUP_BANKS[:g]) for g in range(N_GROUPS)]
 MAX_BANKS = max(GROUP_BANKS)
 REGROUP_LAG, QUANTISE_LAG, CLAMP_LAG, SQUARE_LAG, ROOT_LAG, ADD_LAG = 1, 2, 3, 4, 6, 9
 SCALAR_BANKS = 8
-VECTOR_COLS = 416
+VECTOR_COLS = 384
 OVERLAP = 8
 GPSIMD_GROUPS = 11
 TENSOR_ADD_GROUPS = 2
@@ -214,9 +214,9 @@ def tile_hgatmodel_t_kernel(tc, h, out):
             run(transpose_users, step)
             if step == 0:
                 item_codes, item_scales = prepare_items()
+            run(add_theta, step - ADD_LAG)
             run(quantise_users, step - QUANTISE_LAG)
             run(multiply, step - QUANTISE_LAG)
-            run(add_theta, step - ADD_LAG)
             run(root, step - ROOT_LAG)
             run(regroup_users, step - REGROUP_LAG)
             run(clamp, step - CLAMP_LAG)

@@ -28,9 +28,10 @@ N_GROUPS = len(GROUP_BANKS)
 FIRST_BANK = [sum(GROUP_BANKS[:g]) for g in range(N_GROUPS)]
 MAX_BANKS = max(GROUP_BANKS)
 REGROUP_LAG, QUANTISE_LAG, CLAMP_LAG, SQUARE_LAG, ROOT_LAG, ADD_LAG = 1, 2, 3, 4, 6, 9
-SCALAR_BANKS = 8
+SCALAR_BANKS = 10
 VECTOR_COLS = 384
 OVERLAP = 8
+GPSIMD_SQUARE_GROUPS = range(3, 6)
 GPSIMD_GROUPS = 11
 TENSOR_ADD_GROUPS = 2
 CLOCK_COLS = 96
@@ -175,7 +176,11 @@ def tile_hgatmodel_t_kernel(tc, h, out):
                     theta = theta_of[g][:, cols]
                     nc.vector.tensor_tensor(out=root_of[g][:, cols], in0=theta, in1=theta, op=ALU.mult)
             else:
-                nc.scalar.activation(out=root_of[g][:], in_=theta_of[g][:], func=ACT.Square)
+                ours = BANK_COLS if g in GPSIMD_SQUARE_GROUPS else GROUP_BANKS[g] * BANK_COLS
+                nc.scalar.activation(out=root_of[g][:, 0:ours], in_=theta_of[g][:, 0:ours], func=ACT.Square)
+                if g in GPSIMD_SQUARE_GROUPS:
+                    theta = theta_of[g][:, ours:]
+                    nc.gpsimd.tensor_tensor(out=root_of[g][:, ours:], in0=theta, in1=theta, op=ALU.mult)
 
         def root(g):
             nc.scalar.activation(out=root_of[g][:], in_=root_of[g][:], func=ACT.Sqrt, bias=minus_one[:], scale=1.0)

@@ -34,8 +34,7 @@ OVERLAP = 8
 GPSIMD_SQUARE_GROUPS = range(3, 6)
 GPSIMD_GROUPS = 11
 TENSOR_ADD_GROUPS = 2
-CLOCK_COLS = 96
-CLOCK_FIRST_GROUP = 5
+CLOCK_FIRST_GROUP = 4
 CLOCK_WARM_UPS = 3
 VECTOR_SQUARE_GROUPS = 1
 END_COLS = 256
@@ -83,15 +82,11 @@ def tile_hgatmodel_t_kernel(tc, h, out):
         table_warmer = consts.tile([P, 1], F32)
         nc.scalar.activation(out=table_warmer[:], in_=minus_one[:], func=ACT.Sqrt, scale=-1.0)
 
-        def transpose_tiles(source, n_tiles, clock=False):
+        def transpose_tiles(source, n_tiles):
             words = source[:].bitcast(F32)
             banks = []
             for b in range(n_tiles // TILES_PER_BANK):
                 bank = flipped.tile([P, TILES_PER_BANK, HALVES, P], F32, name="bank")
-                if clock and b == 0:
-                    nc.tensor.matmul(
-                        bank[:, 0, 0, 0:CLOCK_COLS], lhsT=identity[:], rhs=identity[:, 0:CLOCK_COLS], start=True, stop=True
-                    )
                 for t in range(TILES_PER_BANK):
                     for u in range(HALVES):
                         first = (b * TILES_PER_BANK + t) * WORDS
@@ -126,7 +121,7 @@ def tile_hgatmodel_t_kernel(tc, h, out):
         result_of, sum_of = {}, {}
 
         def transpose_users(g):
-            banks_of[g] = transpose_tiles(user_rows[g], GROUP_BANKS[g] * TILES_PER_BANK, g >= CLOCK_FIRST_GROUP)
+            banks_of[g] = transpose_tiles(user_rows[g], GROUP_BANKS[g] * TILES_PER_BANK)
 
         def regroup_users(g):
             grouped_of[g] = stage.tile([P, GROUP_BANKS[g] * BANK_ROWS], BF16, name="grouped", align_bytes=64)
@@ -143,6 +138,8 @@ def tile_hgatmodel_t_kernel(tc, h, out):
             product_of[g] = []
             for b in range(GROUP_BANKS[g]):
                 bank = products.tile([P, TILES_PER_BANK, ITEMS], F32, name="product")
+                if b == 0 and g >= CLOCK_FIRST_GROUP:
+                    nc.tensor.matmul(bank[:, 0, 0:P], lhsT=identity[:], rhs=identity[:], start=True, stop=True)
                 for t in range(TILES_PER_BANK):
                     cols = slice((b * TILES_PER_BANK + t) * P, (b * TILES_PER_BANK + t + 1) * P)
                     nc.tensor.matmul_mx(

@@ -27,16 +27,13 @@ GROUP_BANKS = [1, 1] + [2] * (USER_TILES // TILES_PER_BANK // 2 - 1)
 N_GROUPS = len(GROUP_BANKS)
 FIRST_BANK = [sum(GROUP_BANKS[:g]) for g in range(N_GROUPS)]
 MAX_BANKS = max(GROUP_BANKS)
-REGROUP_LAG, QUANTISE_LAG, CLAMP_LAG, SQUARE_LAG, ROOT_LAG, ADD_LAG = 1, 2, 3, 4, 6, 9
+REGROUP_LAG, QUANTISE_LAG, CLAMP_LAG, SQUARE_LAG, ROOT_LAG = 1, 2, 4, 5, 6
 SCALAR_BANKS = 10
-VECTOR_COLS = 384
-OVERLAP = 8
-GPSIMD_SQUARE_GROUPS = range(3, 6)
-GPSIMD_GROUPS = 11
-TENSOR_ADD_GROUPS = 2
+GPSIMD_COLS = 608
 CLOCK_FIRST_GROUP = 4
 CLOCK_WARM_UPS = 3
 VECTOR_SQUARE_GROUPS = 1
+PSUM_HALF = 4
 END_COLS = 256
 
 THETA_MIN = 1.0 + 1e-7
@@ -54,11 +51,10 @@ def tile_hgatmodel_t_kernel(tc, h, out):
         consts = ctx.enter_context(tc.tile_pool(name="consts", bufs=1))
         rows = ctx.enter_context(tc.tile_pool(name="rows", bufs=1))
         stage = ctx.enter_context(tc.tile_pool(name="stage", bufs=3))
-        thetas = ctx.enter_context(tc.tile_pool(name="thetas", bufs=ADD_LAG - CLAMP_LAG + 2))
-        roots = ctx.enter_context(tc.tile_pool(name="roots", bufs=ADD_LAG - SQUARE_LAG + 2))
-        results = ctx.enter_context(tc.tile_pool(name="results", bufs=1))
-        flipped = ctx.enter_context(tc.psum_pool(name="flipped", bufs=4))
-        products = ctx.enter_context(tc.psum_pool(name="products", bufs=4))
+        thetas = ctx.enter_context(tc.tile_pool(name="thetas", bufs=1))
+        roots = ctx.enter_context(tc.tile_pool(name="roots", bufs=1))
+        flipped = ctx.enter_context(tc.psum_pool(name="flipped", bufs=PSUM_HALF))
+        products = ctx.enter_context(tc.psum_pool(name="products", bufs=PSUM_HALF))
         ctx.enter_context(tc.manual_schedule())
 
         item_rows = consts.tile([P, ITEM_TILES * COORDS], BF16)
@@ -75,8 +71,6 @@ def tile_hgatmodel_t_kernel(tc, h, out):
         warm_up = flipped.tile([P, TILES_PER_BANK, HALVES, P], F32, name="bank")
         for i in range(CLOCK_WARM_UPS):
             nc.tensor.matmul(warm_up[:, 0, i % HALVES, :], lhsT=identity[:], rhs=identity[:], start=True, stop=True)
-        minus_identity = consts.tile([P, P], F32)
-        nc.vector.tensor_scalar(out=minus_identity[:], in0=identity[:], scalar1=-1.0, scalar2=None, op0=ALU.mult)
         minus_one = consts.tile([P, 1], F32)
         nc.vector.memset(minus_one[:], -1.0)
         table_warmer = consts.tile([P, 1], F32)
@@ -110,15 +104,14 @@ def tile_hgatmodel_t_kernel(tc, h, out):
             return codes, scales
 
         def prepare_items():
-            first_coord = item_rows[:].rearrange("p (j d) -> p j d", j=ITEM_TILES)[:, :, 0:1]
-            nc.vector.tensor_scalar(out=first_coord, in0=first_coord, scalar1=-1.0, scalar2=None, op0=ALU.mult)
+            others = item_rows[:].rearrange("p (j d) -> p j d", j=ITEM_TILES)[:, :, 1:COORDS]
+            nc.vector.tensor_scalar(out=others, in0=others, scalar1=-1.0, scalar2=None, op0=ALU.mult)
             bank = transpose_tiles(item_rows, ITEM_TILES)[0]
             grouped = consts.tile([P, ITEM_TILES * COORDS], BF16, name="item_grouped", align_bytes=64)
             regroup(nc.vector.tensor_copy, bank, grouped, 0)
             return quantise(consts, grouped, ITEM_TILES)
 
         banks_of, grouped_of, quantised_of, product_of, theta_of, root_of = {}, {}, {}, {}, {}, {}
-        result_of, sum_of = {}, {}
 
         def transpose_users(g):
             banks_of[g] = transpose_tiles(user_rows[g], GROUP_BANKS[g] * TILES_PER_BANK)
@@ -135,99 +128,97 @@ def tile_hgatmodel_t_kernel(tc, h, out):
 
         def multiply(g):
             codes, scales = quantised_of[g]
+            n_users = GROUP_BANKS[g] * TILES_PER_BANK * P
+            halves_per_bank = BANK_COLS // n_users
             product_of[g] = []
             for b in range(GROUP_BANKS[g]):
-                bank = products.tile([P, TILES_PER_BANK, ITEMS], F32, name="product")
+                bank = products.tile([P, BANK_COLS], F32, name="product")
                 if b == 0 and g >= CLOCK_FIRST_GROUP:
-                    nc.tensor.matmul(bank[:, 0, 0:P], lhsT=identity[:], rhs=identity[:], start=True, stop=True)
-                for t in range(TILES_PER_BANK):
-                    cols = slice((b * TILES_PER_BANK + t) * P, (b * TILES_PER_BANK + t + 1) * P)
+                    nc.tensor.matmul(bank[:, 0:P], lhsT=identity[:], rhs=identity[:], start=True, stop=True)
+                for i in range(halves_per_bank):
+                    half = b * halves_per_bank + i
+                    items = slice(half * P, (half + 1) * P)
                     nc.tensor.matmul_mx(
-                        out=bank[:, t, :],
-                        lhsT=codes[:, cols].bitcast(FP8X4),
-                        lhsT_scale=scales[:, cols],
-                        rhs=item_codes[:].bitcast(FP8X4),
-                        rhs_scale=item_scales[:],
+                        out=bank[:, i * n_users : (i + 1) * n_users],
+                        lhsT=item_codes[:, items].bitcast(FP8X4),
+                        lhsT_scale=item_scales[:, items],
+                        rhs=codes[:].bitcast(FP8X4),
+                        rhs_scale=scales[:],
                         start=True,
                         stop=True,
                     )
                 product_of[g].append(bank)
 
         def clamp(g):
-            theta_of[g] = thetas.tile([P, GROUP_BANKS[g] * BANK_COLS], F32, name="minus_theta")
+            theta_of[g] = thetas.tile([P, GROUP_BANKS[g] * BANK_COLS], F32, name="theta%d" % g)
             for b in range(GROUP_BANKS[g]):
                 nc.vector.tensor_scalar(
                     out=theta_of[g][:, b * BANK_COLS : (b + 1) * BANK_COLS],
-                    in0=product_of[g][b][:].rearrange("p t i -> p (t i)"),
-                    scalar1=-THETA_MIN,
-                    scalar2=-THETA_MAX,
-                    op0=ALU.min,
-                    op1=ALU.max,
+                    in0=product_of[g][b][:],
+                    scalar1=THETA_MIN,
+                    scalar2=THETA_MAX,
+                    op0=ALU.max,
+                    op1=ALU.min,
                 )
 
-        def square(g):
-            root_of[g] = roots.tile([P, GROUP_BANKS[g] * BANK_COLS], F32, name="root")
+        def square_parts(g):
+            cols = GROUP_BANKS[g] * BANK_COLS
             if g >= N_GROUPS - VECTOR_SQUARE_GROUPS:
-                for b in range(GROUP_BANKS[g]):
-                    cols = slice(b * BANK_COLS, (b + 1) * BANK_COLS)
-                    theta = theta_of[g][:, cols]
-                    nc.vector.tensor_tensor(out=root_of[g][:, cols], in0=theta, in1=theta, op=ALU.mult)
-            else:
-                ours = BANK_COLS if g in GPSIMD_SQUARE_GROUPS else GROUP_BANKS[g] * BANK_COLS
-                nc.scalar.activation(out=root_of[g][:, 0:ours], in_=theta_of[g][:, 0:ours], func=ACT.Square)
-                if g in GPSIMD_SQUARE_GROUPS:
-                    theta = theta_of[g][:, ours:]
-                    nc.gpsimd.tensor_tensor(out=root_of[g][:, ours:], in0=theta, in1=theta, op=ALU.mult)
+                return (0, 0), (0, 0), (0, cols)
+            if GROUP_BANKS[g] < MAX_BANKS:
+                return (0, cols), (0, 0), (0, 0)
+            return (0, cols - GPSIMD_COLS), (cols - GPSIMD_COLS, cols), (0, 0)
+
+        def square_early(g):
+            root_of[g] = roots.tile([P, GROUP_BANKS[g] * BANK_COLS], F32, name="root%d" % g)
+            scalar_part, gpsimd_part, vector_part = square_parts(g)
+            for engine, (first, last) in ((nc.gpsimd, gpsimd_part), (nc.vector, vector_part)):
+                if last > first:
+                    theta = theta_of[g][:, first:last]
+                    engine.tensor_tensor(out=root_of[g][:, first:last], in0=theta, in1=theta, op=ALU.mult)
+
+        def square(g):
+            first, last = square_parts(g)[0]
+            if last > first:
+                nc.scalar.activation(out=root_of[g][:, first:last], in_=theta_of[g][:, first:last], func=ACT.Square)
 
         def root(g):
             nc.scalar.activation(out=root_of[g][:], in_=root_of[g][:], func=ACT.Sqrt, bias=minus_one[:], scale=1.0)
-
-        def add_theta(g):
-            cols = GROUP_BANKS[g] * BANK_COLS
-            result_of[g] = results.tile([P, cols], F32, name="result%d" % g)
-            if g >= N_GROUPS - TENSOR_ADD_GROUPS:
-                return
-            shared = GROUP_BANKS[g] == MAX_BANKS and g < GPSIMD_GROUPS
-            parts = [(nc.vector, 0, VECTOR_COLS + OVERLAP if shared else cols)]
-            if shared:
-                parts.append((nc.gpsimd, VECTOR_COLS, cols))
-            for engine, first, last in parts:
-                engine.tensor_tensor(
-                    out=result_of[g][:, first:last],
-                    in0=root_of[g][:, first:last],
-                    in1=theta_of[g][:, first:last],
-                    op=ALU.subtract,
-                )
-
-        def add_on_tensor(g):
-            for b in range(GROUP_BANKS[g]):
-                pool = flipped if b == 0 else products
-                bank = pool.tile([P, BANK_COLS], F32, name="bank" if b == 0 else "product")
-                cols = slice(b * BANK_COLS, (b + 1) * BANK_COLS)
-                nc.tensor.matmul(bank[:], lhsT=minus_identity[:], rhs=theta_of[g][:, cols], start=True, stop=False)
-                nc.tensor.matmul(bank[:], lhsT=identity[:], rhs=root_of[g][:, cols], start=False, stop=True)
-                sum_of[(g, b)] = bank
 
         def run(stage_fn, g):
             if 0 <= g < N_GROUPS:
                 stage_fn(g)
 
-        for step in range(N_GROUPS + ADD_LAG):
-            run(transpose_users, step)
+        for step in range(N_GROUPS + ROOT_LAG):
             if step == 0:
+                run(transpose_users, step)
                 item_codes, item_scales = prepare_items()
-            run(add_theta, step - ADD_LAG)
+            run(clamp, step - CLAMP_LAG)
+            run(square_early, step - CLAMP_LAG)
             run(quantise_users, step - QUANTISE_LAG)
             run(multiply, step - QUANTISE_LAG)
-            run(root, step - ROOT_LAG)
+            if step > 0:
+                run(transpose_users, step)
             run(regroup_users, step - REGROUP_LAG)
-            run(clamp, step - CLAMP_LAG)
-            if step - CLAMP_LAG >= N_GROUPS - VECTOR_SQUARE_GROUPS:
-                run(square, step - CLAMP_LAG)
-            if step - SQUARE_LAG < N_GROUPS - VECTOR_SQUARE_GROUPS:
-                run(square, step - SQUARE_LAG)
-        for g in range(N_GROUPS - TENSOR_ADD_GROUPS, N_GROUPS):
-            add_on_tensor(g)
+            run(square, step - SQUARE_LAG)
+            run(root, step - ROOT_LAG)
+
+        def add_on_tensor(g, b, pool, name):
+            n_users = GROUP_BANKS[g] * TILES_PER_BANK * P
+            bank = pool.tile([P, TILES_PER_BANK, ITEM_TILES, P], F32, name=name)
+            for t in range(TILES_PER_BANK):
+                for j in range(ITEM_TILES):
+                    first = j * n_users + (b * TILES_PER_BANK + t) * P
+                    for source, is_first in ((theta_of[g], True), (root_of[g], False)):
+                        nc.tensor.matmul(
+                            bank[:, t, j, :],
+                            lhsT=source[:, first : first + P],
+                            rhs=identity[:],
+                            start=is_first,
+                            stop=not is_first,
+                            is_transpose=True,
+                        )
+            return bank[:].rearrange("p t j i -> p (t j i)")
 
         def pieces(g):
             cols = GROUP_BANKS[g] * BANK_COLS
@@ -239,19 +230,21 @@ def tile_hgatmodel_t_kernel(tc, h, out):
             return list(zip(cuts[:-1], cuts[1:]))
 
         for g in range(N_GROUPS):
+            result = rows.tile([P, GROUP_BANKS[g] * BANK_COLS], F32, name="user_rows%d" % g)
+            sums = []
+            for b in range(GROUP_BANKS[g]):
+                in_flipped = (FIRST_BANK[g] + b) // PSUM_HALF % 2 == 0
+                pool, name = (flipped, "bank") if in_flipped else (products, "product")
+                sums.append(add_on_tensor(g, b, pool, name))
             for first, last in pieces(g):
                 for start in range(first, last, BANK_COLS):
                     stop = min(start + BANK_COLS, last)
-                    part = result_of[g][:, start:stop]
-                    source = part
-                    if g >= N_GROUPS - TENSOR_ADD_GROUPS:
-                        b = start // BANK_COLS
-                        source = sum_of[(g, b)][:, start - b * BANK_COLS : stop - b * BANK_COLS]
+                    part = result[:, start:stop]
+                    b = start // BANK_COLS
+                    source = sums[b][:, start - b * BANK_COLS : stop - b * BANK_COLS]
                     nc.scalar.activation(out=part, in_=source, func=ACT.Ln)
                     nc.vector.scalar_tensor_tensor(
                         out=part, in0=part, scalar=-1.0, in1=part, op0=ALU.mult, op1=ALU.mult
                     )
                 offset = FIRST_BANK[g] * BANK_COLS
-                nc.sync.dma_start(
-                    out=result_out[:, offset + first : offset + last], in_=result_of[g][:, first:last]
-                )
+                nc.sync.dma_start(out=result_out[:, offset + first : offset + last], in_=result[:, first:last])

@@ -28,10 +28,11 @@ N_GROUPS = len(GROUP_BANKS)
 FIRST_BANK = [sum(GROUP_BANKS[:g]) for g in range(N_GROUPS)]
 MAX_BANKS = max(GROUP_BANKS)
 REGROUP_LAG, QUANTISE_LAG, CLAMP_LAG, SQUARE_LAG, ROOT_LAG = 1, 2, 4, 5, 6
-SCALAR_BANKS = 10
+SCALAR_BANKS = 12
 GPSIMD_COLS = 608
 CLOCK_FIRST_GROUP = 4
 CLOCK_WARM_UPS = 3
+CLOCK_ROOTS, CLOCK_PER_ROOT = 3, 2
 VECTOR_SQUARE_GROUPS = 1
 PSUM_HALF = 4
 END_COLS = 256
@@ -190,22 +191,25 @@ def tile_hgatmodel_t_kernel(tc, h, out):
                 stage_fn(g)
 
         for step in range(N_GROUPS + ROOT_LAG):
+            run(transpose_users, step)
             if step == 0:
-                run(transpose_users, step)
                 item_codes, item_scales = prepare_items()
             run(clamp, step - CLAMP_LAG)
             run(square_early, step - CLAMP_LAG)
             run(quantise_users, step - QUANTISE_LAG)
             run(multiply, step - QUANTISE_LAG)
-            if step > 0:
-                run(transpose_users, step)
             run(regroup_users, step - REGROUP_LAG)
             run(square, step - SQUARE_LAG)
             run(root, step - ROOT_LAG)
 
-        def add_on_tensor(g, b, pool, name):
+        def add_on_tensor(g, b, pool, name, clock_group):
             n_users = GROUP_BANKS[g] * TILES_PER_BANK * P
             bank = pool.tile([P, TILES_PER_BANK, ITEM_TILES, P], F32, name=name)
+            if clock_group is not None:
+                for i in range(CLOCK_PER_ROOT):
+                    nc.tensor.matmul(
+                        bank[:, 0, i, :], lhsT=root_of[clock_group][:, 0:P], rhs=identity[:], start=True, stop=True
+                    )
             for t in range(TILES_PER_BANK):
                 for j in range(ITEM_TILES):
                     first = j * n_users + (b * TILES_PER_BANK + t) * P
@@ -229,13 +233,14 @@ def tile_hgatmodel_t_kernel(tc, h, out):
                 cuts = [0] + list(range(cols - BANK_COLS, cols + 1, END_COLS))
             return list(zip(cuts[:-1], cuts[1:]))
 
+        clock_groups = {2 * i + 2: N_GROUPS - CLOCK_ROOTS + i for i in range(CLOCK_ROOTS)}
         for g in range(N_GROUPS):
             result = rows.tile([P, GROUP_BANKS[g] * BANK_COLS], F32, name="user_rows%d" % g)
             sums = []
             for b in range(GROUP_BANKS[g]):
                 in_flipped = (FIRST_BANK[g] + b) // PSUM_HALF % 2 == 0
                 pool, name = (flipped, "bank") if in_flipped else (products, "product")
-                sums.append(add_on_tensor(g, b, pool, name))
+                sums.append(add_on_tensor(g, b, pool, name, clock_groups.get(FIRST_BANK[g] + b)))
             for first, last in pieces(g):
                 for start in range(first, last, BANK_COLS):
                     stop = min(start + BANK_COLS, last)

@@ -29,7 +29,9 @@ FIRST_BANK = [sum(GROUP_BANKS[:g]) for g in range(N_GROUPS)]
 MAX_BANKS = max(GROUP_BANKS)
 REGROUP_LAG, QUANTISE_LAG, CLAMP_LAG, SQUARE_LAG, ROOT_LAG = 1, 2, 4, 5, 6
 SCALAR_BANKS = 12
-GPSIMD_COLS = 608
+GPSIMD_COLS = 576
+GPSIMD_END_COLS = 384
+VECTOR_ADD_GROUPS = range(0, 4)
 CLOCK_FIRST_GROUP = 4
 CLOCK_WARM_UPS = 3
 CLOCK_ROOTS, CLOCK_PER_ROOT = 3, 2
@@ -128,23 +130,25 @@ def tile_hgatmodel_t_kernel(tc, h, out):
             quantised_of[g] = quantise(stage, grouped_of[g], GROUP_BANKS[g] * TILES_PER_BANK)
 
         def multiply(g):
-            codes, scales = quantised_of[g]
+            users, items = quantised_of[g], (item_codes, item_scales)
             n_users = GROUP_BANKS[g] * TILES_PER_BANK * P
-            halves_per_bank = BANK_COLS // n_users
+            on_partitions, along_free, free_size = items, users, n_users
+            if g in VECTOR_ADD_GROUPS:
+                on_partitions, along_free, free_size = users, items, ITEMS
+            per_bank = BANK_COLS // free_size
             product_of[g] = []
             for b in range(GROUP_BANKS[g]):
                 bank = products.tile([P, BANK_COLS], F32, name="product")
                 if b == 0 and g >= CLOCK_FIRST_GROUP:
                     nc.tensor.matmul(bank[:, 0:P], lhsT=identity[:], rhs=identity[:], start=True, stop=True)
-                for i in range(halves_per_bank):
-                    half = b * halves_per_bank + i
-                    items = slice(half * P, (half + 1) * P)
+                for i in range(per_bank):
+                    rows_128 = slice((b * per_bank + i) * P, (b * per_bank + i + 1) * P)
                     nc.tensor.matmul_mx(
-                        out=bank[:, i * n_users : (i + 1) * n_users],
-                        lhsT=item_codes[:, items].bitcast(FP8X4),
-                        lhsT_scale=item_scales[:, items],
-                        rhs=codes[:].bitcast(FP8X4),
-                        rhs_scale=scales[:],
+                        out=bank[:, i * free_size : (i + 1) * free_size],
+                        lhsT=on_partitions[0][:, rows_128].bitcast(FP8X4),
+                        lhsT_scale=on_partitions[1][:, rows_128],
+                        rhs=along_free[0][:].bitcast(FP8X4),
+                        rhs_scale=along_free[1][:],
                         start=True,
                         stop=True,
                     )
@@ -168,7 +172,8 @@ def tile_hgatmodel_t_kernel(tc, h, out):
                 return (0, 0), (0, 0), (0, cols)
             if GROUP_BANKS[g] < MAX_BANKS:
                 return (0, cols), (0, 0), (0, 0)
-            return (0, cols - GPSIMD_COLS), (cols - GPSIMD_COLS, cols), (0, 0)
+            ours = cols - (GPSIMD_END_COLS if g == N_GROUPS - 1 - VECTOR_SQUARE_GROUPS else GPSIMD_COLS)
+            return (0, ours), (ours, cols), (0, 0)
 
         def square_early(g):
             root_of[g] = roots.tile([P, GROUP_BANKS[g] * BANK_COLS], F32, name="root%d" % g)
@@ -233,14 +238,24 @@ def tile_hgatmodel_t_kernel(tc, h, out):
                 cuts = [0] + list(range(cols - BANK_COLS, cols + 1, END_COLS))
             return list(zip(cuts[:-1], cuts[1:]))
 
-        clock_groups = {2 * i + 2: N_GROUPS - CLOCK_ROOTS + i for i in range(CLOCK_ROOTS)}
+        result_of = {}
         for g in range(N_GROUPS):
-            result = rows.tile([P, GROUP_BANKS[g] * BANK_COLS], F32, name="user_rows%d" % g)
+            result_of[g] = rows.tile([P, GROUP_BANKS[g] * BANK_COLS], F32, name="user_rows%d" % g)
+            if g in VECTOR_ADD_GROUPS:
+                nc.vector.tensor_tensor(out=result_of[g][:], in0=root_of[g][:], in1=theta_of[g][:], op=ALU.add)
+        clock_groups = {2 * i + 2: N_GROUPS - CLOCK_ROOTS + i for i in range(CLOCK_ROOTS)}
+        n_sum_banks = 0
+        for g in range(N_GROUPS):
+            result = result_of[g]
             sums = []
             for b in range(GROUP_BANKS[g]):
-                in_flipped = (FIRST_BANK[g] + b) // PSUM_HALF % 2 == 0
+                if g in VECTOR_ADD_GROUPS:
+                    sums.append(result[:, b * BANK_COLS : (b + 1) * BANK_COLS])
+                    continue
+                in_flipped = n_sum_banks // PSUM_HALF % 2 == 0
                 pool, name = (flipped, "bank") if in_flipped else (products, "product")
-                sums.append(add_on_tensor(g, b, pool, name, clock_groups.get(FIRST_BANK[g] + b)))
+                sums.append(add_on_tensor(g, b, pool, name, clock_groups.get(n_sum_banks)))
+                n_sum_banks += 1
             for first, last in pieces(g):
                 for start in range(first, last, BANK_COLS):
                     stop = min(start + BANK_COLS, last)

import math
from contextlib import ExitStack

import concourse.mybir as mybir
from concourse.masks import make_identity

F32 = mybir.dt.float32
BF16 = mybir.dt.bfloat16
U32 = mybir.dt.uint32
U8 = mybir.dt.uint8
FP8X4 = mybir.dt.float8_e4m3fn_x4
ALU = mybir.AluOpType
ACT = mybir.ActivationFunctionType

P = 128
USERS, ITEMS, COORDS = 8192, 256, 512
FLOPS = 2 * USERS * ITEMS * COORDS

WORDS = COORDS // 2
HALVES = WORDS // P
USER_TILES = USERS // P
ITEM_TILES = ITEMS // P
TILES_PER_BANK = 2
BANK_ROWS = TILES_PER_BANK * COORDS
BANK_COLS = TILES_PER_BANK * ITEMS
GROUP_BANKS = [1, 1] + [2] * (USER_TILES // TILES_PER_BANK // 2 - 1)
N_GROUPS = len(GROUP_BANKS)
FIRST_BANK = [sum(GROUP_BANKS[:g]) for g in range(N_GROUPS)]
MAX_BANKS = max(GROUP_BANKS)
REGROUP_LAG, QUANTISE_LAG, CLAMP_LAG, SQUARE_LAG, ROOT_LAG = 1, 2, 4, 5, 6
SCALAR_BANKS = 12
GPSIMD_COLS = 576
GPSIMD_END_COLS = 384
VECTOR_ADD_GROUPS = range(0, 4)
CLOCK_FIRST_GROUP = 4
CLOCK_WARM_UPS = 3
CLOCK_ROOTS, CLOCK_PER_ROOT = 3, 2
VECTOR_SQUARE_GROUPS = 1
PSUM_HALF = 4
END_COLS = 256

THETA_MIN = 1.0 + 1e-7
MAX_SQDIST = 50.0
THETA_MAX = 0.5 * (math.exp(math.sqrt(MAX_SQDIST)) + math.exp(-math.sqrt(MAX_SQDIST)))


def tile_hgatmodel_t_kernel(tc, h, out):
    nc = tc.nc
    users_in = h[0:USERS, :].rearrange("(p t) d -> p (t d)", t=USER_TILES)
    items_in = h[USERS : USERS + ITEMS, :].rearrange("(j p) d -> p j d", p=P)
    result_out = out.rearrange("(p t) i -> p (t i)", t=USER_TILES)

    with ExitStack() as ctx:
        consts = ctx.enter_context(tc.tile_pool(name="consts", bufs=1))
        rows = ctx.enter_context(tc.tile_pool(name="rows", bufs=1))
        stage = ctx.enter_context(tc.tile_pool(name="stage", bufs=3))
        thetas = ctx.enter_context(tc.tile_pool(name="thetas", bufs=1))
        roots = ctx.enter_context(tc.tile_pool(name="roots", bufs=1))
        flipped = ctx.enter_context(tc.psum_pool(name="flipped", bufs=PSUM_HALF))
        products = ctx.enter_context(tc.psum_pool(name="products", bufs=PSUM_HALF))
        ctx.enter_context(tc.manual_schedule())

        item_rows = consts.tile([P, ITEM_TILES * COORDS], BF16)
        user_rows = {}
        for g in range(N_GROUPS):
            first, width = FIRST_BANK[g] * BANK_ROWS, GROUP_BANKS[g] * BANK_ROWS
            user_rows[g] = rows.tile([P, width], BF16, name="user_rows%d" % g)
            nc.sync.dma_start(out=user_rows[g][:], in_=users_in[:, first : first + width])
            if g == 0:
                nc.sync.dma_start(out=item_rows[:].rearrange("p (j d) -> p j d", j=ITEM_TILES), in_=items_in)

        identity = consts.tile([P, P], F32)
        make_identity(nc, identity[:])
        warm_up = flipped.tile([P, TILES_PER_BANK, HALVES, P], F32, name="bank")
        for i in range(CLOCK_WARM_UPS):
            nc.tensor.matmul(warm_up[:, 0, i % HALVES, :], lhsT=identity[:], rhs=identity[:], start=True, stop=True)
        minus_one = consts.tile([P, 1], F32)
        nc.vector.memset(minus_one[:], -1.0)
        table_warmer = consts.tile([P, 1], F32)
        nc.scalar.activation(out=table_warmer[:], in_=minus_one[:], func=ACT.Sqrt, scale=-1.0)

        def transpose_tiles(source, n_tiles):
            words = source[:].bitcast(F32)
            banks = []
            for b in range(n_tiles // TILES_PER_BANK):
                bank = flipped.tile([P, TILES_PER_BANK, HALVES, P], F32, name="bank")
                for t in range(TILES_PER_BANK):
                    for u in range(HALVES):
                        first = (b * TILES_PER_BANK + t) * WORDS
                        nc.tensor.transpose(
                            bank[:, t, u, :], words[:, first + u : first + WORDS : HALVES], identity[:]
                        )
                banks.append(bank)
            return banks

        def regroup(copy, bank, grouped, b):
            as_words = grouped[:].bitcast(F32).rearrange("p (t r u) -> p t r u", r=P, u=HALVES)
            copy(
                out=as_words[:, b * TILES_PER_BANK : (b + 1) * TILES_PER_BANK],
                in_=bank[:].rearrange("p t u r -> p t r u"),
            )

        def quantise(pool, grouped, n_tiles):
            codes = pool.tile([P, n_tiles * P], U32, name="codes%d" % n_tiles, align_bytes=64)
            scales = pool.tile([P, n_tiles * P], U8, name="scales%d" % n_tiles, align_bytes=64)
            nc.vector.quantize_mx(out=codes[:].bitcast(FP8X4), scales=scales[:], in_=grouped[:])
            return codes, scales

        def prepare_items():
            others = item_rows[:].rearrange("p (j d) -> p j d", j=ITEM_TILES)[:, :, 1:COORDS]
            nc.vector.tensor_scalar(out=others, in0=others, scalar1=-1.0, scalar2=None, op0=ALU.mult)
            bank = transpose_tiles(item_rows, ITEM_TILES)[0]
            grouped = consts.tile([P, ITEM_TILES * COORDS], BF16, name="item_grouped", align_bytes=64)
            regroup(nc.vector.tensor_copy, bank, grouped, 0)
            return quantise(consts, grouped, ITEM_TILES)

        banks_of, grouped_of, quantised_of, product_of, theta_of, root_of = {}, {}, {}, {}, {}, {}

        def transpose_users(g):
            banks_of[g] = transpose_tiles(user_rows[g], GROUP_BANKS[g] * TILES_PER_BANK)

        def regroup_users(g):
            grouped_of[g] = stage.tile([P, GROUP_BANKS[g] * BANK_ROWS], BF16, name="grouped", align_bytes=64)
            for b in range(GROUP_BANKS[g]):
                bank_index = FIRST_BANK[g] + b
                on_vector = bank_index >= SCALAR_BANKS and bank_index % 2 == 0
                regroup(nc.vector.tensor_copy if on_vector else nc.scalar.copy, banks_of[g][b], grouped_of[g], b)

        def quantise_users(g):
            quantised_of[g] = quantise(stage, grouped_of[g], GROUP_BANKS[g] * TILES_PER_BANK)

        def multiply(g):
            users, items = quantised_of[g], (item_codes, item_scales)
            n_users = GROUP_BANKS[g] * TILES_PER_BANK * P
            on_partitions, along_free, free_size = items, users, n_users
            if g in VECTOR_ADD_GROUPS:
                on_partitions, along_free, free_size = users, items, ITEMS
            per_bank = BANK_COLS // free_size
            product_of[g] = []
            for b in range(GROUP_BANKS[g]):
                bank = products.tile([P, BANK_COLS], F32, name="product")
                if b == 0 and g >= CLOCK_FIRST_GROUP:
                    nc.tensor.matmul(bank[:, 0:P], lhsT=identity[:], rhs=identity[:], start=True, stop=True)
                for i in range(per_bank):
                    rows_128 = slice((b * per_bank + i) * P, (b * per_bank + i + 1) * P)
                    nc.tensor.matmul_mx(
                        out=bank[:, i * free_size : (i + 1) * free_size],
                        lhsT=on_partitions[0][:, rows_128].bitcast(FP8X4),
                        lhsT_scale=on_partitions[1][:, rows_128],
                        rhs=along_free[0][:].bitcast(FP8X4),
                        rhs_scale=along_free[1][:],
                        start=True,
                        stop=True,
                    )
                product_of[g].append(bank)

        def clamp(g):
            theta_of[g] = thetas.tile([P, GROUP_BANKS[g] * BANK_COLS], F32, name="theta%d" % g)
            for b in range(GROUP_BANKS[g]):
                nc.vector.tensor_scalar(
                    out=theta_of[g][:, b * BANK_COLS : (b + 1) * BANK_COLS],
                    in0=product_of[g][b][:],
                    scalar1=THETA_MIN,
                    scalar2=THETA_MAX,
                    op0=ALU.max,
                    op1=ALU.min,
                )

        def square_parts(g):
            cols = GROUP_BANKS[g] * BANK_COLS
            if g >= N_GROUPS - VECTOR_SQUARE_GROUPS:
                return (0, 0), (0, 0), (0, cols)
            if GROUP_BANKS[g] < MAX_BANKS:
                return (0, cols), (0, 0), (0, 0)
            ours = cols - (GPSIMD_END_COLS if g == N_GROUPS - 1 - VECTOR_SQUARE_GROUPS else GPSIMD_COLS)
            return (0, ours), (ours, cols), (0, 0)

        def square_early(g):
            root_of[g] = roots.tile([P, GROUP_BANKS[g] * BANK_COLS], F32, name="root%d" % g)
            scalar_part, gpsimd_part, vector_part = square_parts(g)
            for engine, (first, last) in ((nc.gpsimd, gpsimd_part), (nc.vector, vector_part)):
                if last > first:
                    theta = theta_of[g][:, first:last]
                    engine.tensor_tensor(out=root_of[g][:, first:last], in0=theta, in1=theta, op=ALU.mult)

        def square(g):
            first, last = square_parts(g)[0]
            if last > first:
                nc.scalar.activation(out=root_of[g][:, first:last], in_=theta_of[g][:, first:last], func=ACT.Square)

        def root(g):
            nc.scalar.activation(out=root_of[g][:], in_=root_of[g][:], func=ACT.Sqrt, bias=minus_one[:], scale=1.0)

        def run(stage_fn, g):
            if 0 <= g < N_GROUPS:
                stage_fn(g)

        for step in range(N_GROUPS + ROOT_LAG):
            run(transpose_users, step)
            if step == 0:
                item_codes, item_scales = prepare_items()
            run(clamp, step - CLAMP_LAG)
            run(square_early, step - CLAMP_LAG)
            run(quantise_users, step - QUANTISE_LAG)
            run(multiply, step - QUANTISE_LAG)
            run(regroup_users, step - REGROUP_LAG)
            run(square, step - SQUARE_LAG)
            run(root, step - ROOT_LAG)

        def add_on_tensor(g, b, pool, name, clock_group):
            n_users = GROUP_BANKS[g] * TILES_PER_BANK * P
            bank = pool.tile([P, TILES_PER_BANK, ITEM_TILES, P], F32, name=name)
            if clock_group is not None:
                for i in range(CLOCK_PER_ROOT):
                    nc.tensor.matmul(
                        bank[:, 0, i, :], lhsT=root_of[clock_group][:, 0:P], rhs=identity[:], start=True, stop=True
                    )
            for t in range(TILES_PER_BANK):
                for j in range(ITEM_TILES):
                    first = j * n_users + (b * TILES_PER_BANK + t) * P
                    for source, is_first in ((theta_of[g], True), (root_of[g], False)):
                        nc.tensor.matmul(
                            bank[:, t, j, :],
                            lhsT=source[:, first : first + P],
                            rhs=identity[:],
                            start=is_first,
                            stop=not is_first,
                            is_transpose=True,
                        )
            return bank[:].rearrange("p t j i -> p (t j i)")

        def pieces(g):
            cols = GROUP_BANKS[g] * BANK_COLS
            cuts = [0, cols]
            if g == 0:
                cuts = list(range(0, cols + 1, END_COLS))
            if g == N_GROUPS - 1:
                cuts = [0] + list(range(cols - BANK_COLS, cols + 1, END_COLS))
            return list(zip(cuts[:-1], cuts[1:]))

        result_of = {}
        for g in range(N_GROUPS):
            result_of[g] = rows.tile([P, GROUP_BANKS[g] * BANK_COLS], F32, name="user_rows%d" % g)
            if g in VECTOR_ADD_GROUPS:
                nc.vector.tensor_tensor(out=result_of[g][:], in0=root_of[g][:], in1=theta_of[g][:], op=ALU.add)
        clock_groups = {2 * i + 2: N_GROUPS - CLOCK_ROOTS + i for i in range(CLOCK_ROOTS)}
        n_sum_banks = 0
        for g in range(N_GROUPS):
            result = result_of[g]
            sums = []
            for b in range(GROUP_BANKS[g]):
                if g in VECTOR_ADD_GROUPS:
                    sums.append(result[:, b * BANK_COLS : (b + 1) * BANK_COLS])
                    continue
                in_flipped = n_sum_banks // PSUM_HALF % 2 == 0
                pool, name = (flipped, "bank") if in_flipped else (products, "product")
                sums.append(add_on_tensor(g, b, pool, name, clock_groups.get(n_sum_banks)))
                n_sum_banks += 1
            for first, last in pieces(g):
                for start in range(first, last, BANK_COLS):
                    stop = min(start + BANK_COLS, last)
                    part = result[:, start:stop]
                    b = start // BANK_COLS
                    source = sums[b][:, start - b * BANK_COLS : stop - b * BANK_COLS]
                    nc.scalar.activation(out=part, in_=source, func=ACT.Ln)
                    nc.vector.scalar_tensor_tensor(
                        out=part, in0=part, scalar=-1.0, in1=part, op0=ALU.mult, op1=ALU.mult
                    )
                offset = FIRST_BANK[g] * BANK_COLS
                nc.sync.dma_start(out=result_out[:, offset + first : offset + last], in_=result[:, first:last])
